import numpy as np
import ml_dtypes


def mxq(x, axis, fmt="e4m3"):
    dtype, down = {"e4m3": (ml_dtypes.float8_e4m3fn, 7), "e5m2": (ml_dtypes.float8_e5m2, 14)}[fmt]
    v = np.moveaxis(np.asarray(x, np.float32).astype(ml_dtypes.bfloat16).astype(np.float64), axis, -1)
    blocks = v.reshape(v.shape[:-1] + (-1, 32))
    amax = np.abs(blocks).max(-1, keepdims=True)
    byte = np.maximum(np.where(amax > 0, np.frexp(amax)[1] - 1 + 127, 0) - down, 1)
    scale = np.exp2(byte - 127.0)
    codes = (blocks / scale).astype(np.float32).astype(dtype).astype(np.float64)
    return np.moveaxis((codes * scale).reshape(v.shape), -1, axis)


WIDE = False


def mx_kscale(k):
    if not WIDE:
        return np.ones(k)
    levels = np.array([10, -10, 5, -5, 0])
    a = np.random.permutation(np.resize(levels, k // 512 * 4)).reshape(k // 512, 4)
    idx = np.arange(k)
    return np.exp2(a[idx // 512, idx % 128 // 32])


BF16 = ml_dtypes.bfloat16


def bf(x):
    return np.asarray(x, np.float32).astype(BF16)


def f64(x):
    return np.asarray(x).astype(np.float64)


B, N, H, R, L = 2, 512, 512, 10, 2
NEG_INF = -1e30


def setup_inputs():
    s = mx_kscale(H)
    return {"adj": bf(np.random.uniform(size=(B, N, N, R)) * 4.0),
            "x": bf(np.random.standard_normal((B, N, H)) * s),
            "dmask": bf(np.random.uniform(size=(B, 1, N)) > 0.1),
            "W": bf(np.random.standard_normal((R, H, H)) * 1.5 / np.sqrt(H) / s[:, None])}


def reference(adj, x, dmask, W):
    a = f64(adj).transpose(0, 3, 1, 2)
    m = f64(dmask)[:, None, :, :]
    logits = a * m + (1.0 - m) * NEG_INF
    e = np.exp(logits - logits.max(-1, keepdims=True))
    att = e / e.sum(-1, keepdims=True)
    h = mxq(f64(x), 2, "e4m3")[:, None] @ mxq(f64(W), 1, "e4m3")[None]
    g = np.maximum(mxq(att, 3, "e4m3") @ mxq(h, 2, "e4m3"), 0.0)
    return g.sum(1)

@@ -1,0 +1,507 @@
+from contextlib import ExitStack
+
+import concourse.mybir as mybir
+from concourse.masks import make_identity
+
+F32 = mybir.dt.float32
+BF16 = mybir.dt.bfloat16
+U32 = mybir.dt.uint32
+U8 = mybir.dt.uint8
+FP8X4 = mybir.dt.float8_e4m3fn_x4
+ALU = mybir.AluOpType
+AF = mybir.ActivationFunctionType
+
+P = 128
+B, N, H, R = 2, 512, 512, 10
+NT = N // P
+NU = B * NT
+FLOPS = 2 * B * R * N * H * (H + N)
+BIG = 1.0e30
+LPW = 7168
+H_BANKS = 3
+E_AHEAD = 3
+W_AHEAD = 12
+FIXED = {"V": 36.0, "A": 50.0}
+G_BANKS = 3
+S2_PER_STEP = 4
+HEAD_BANKS = (2, 2, 2, 2, 2, 2, 2, 2, 2, 2, 2, 2)
+FRONT_TICKS = ((1, 0, 1, 0, 0, 0), (0, 1, 0, 0, 0, 0), (0, 0, 1, 0, 0, 0), (1, 0, 0, 1, 0, 0), (1, 1, 1, 1, 1, 1))
+
+
+def plane_offset(t):
+    return (t // 4) * 1024 + t % 4
+
+
+def on_vector(kind, idx):
+    if kind == "regroup":
+        return True
+    if kind == "norm":
+        return not (idx >= 50 and idx % 2 == 1)
+    return False
+
+
+def h_rate(j):
+    return 3
+
+
+def tile_rgat_pa_kernel(tc, adj, x, dmask, W, out):
+    nc = tc.nc
+    with ExitStack() as ctx:
+        const = ctx.enter_context(tc.tile_pool(name="const", bufs=1))
+        a_pool = ctx.enter_context(tc.tile_pool(name="a_pool", bufs=2))
+        l_pool = ctx.enter_context(tc.tile_pool(name="l_pool", bufs=2))
+        t_pool = ctx.enter_context(tc.tile_pool(name="t_pool", bufs=1))
+        st_pool = ctx.enter_context(tc.tile_pool(name="st_pool", bufs=3))
+        e_pool = ctx.enter_context(tc.tile_pool(name="e_pool", bufs=E_AHEAD + 1))
+        at_pool = ctx.enter_context(tc.tile_pool(name="at_pool", bufs=3))
+        ga_pool = ctx.enter_context(tc.tile_pool(name="ga_pool", bufs=3))
+        aq_pool = ctx.enter_context(tc.tile_pool(name="aq_pool", bufs=5))
+        w_pool = ctx.enter_context(tc.tile_pool(name="w_pool", bufs=3))
+        gw_pool = ctx.enter_context(tc.tile_pool(name="gw_pool", bufs=2))
+        wq_pool = ctx.enter_context(tc.tile_pool(name="wq_pool", bufs=2))
+        gh_pool = ctx.enter_context(tc.tile_pool(name="gh_pool", bufs=2))
+        acc_pool = ctx.enter_context(tc.tile_pool(name="acc_pool", bufs=5))
+        ps_h = ctx.enter_context(tc.psum_pool(name="ps_h", bufs=H_BANKS))
+        ps_g = ctx.enter_context(tc.psum_pool(name="ps_g", bufs=G_BANKS))
+        ps_t = ctx.enter_context(tc.psum_pool(name="ps_t", bufs=2))
+
+        load = {"V": 0.0, "A": 0.0}
+
+        def busy(eng, cycles):
+            load[eng] += cycles + FIXED[eng]
+
+        def pick(kind, idx):
+            return "V" if on_vector(kind, idx) else "A"
+        warm = const.tile([P, 1], F32, name="warm")
+        nc.vector.memset(warm[:], 0.0)
+        nc.scalar.activation(out=warm[:], in_=warm[:], func=AF.Exp)
+        ident32 = const.tile([P, P], F32, name="ident32")
+        make_identity(nc, ident32[:])
+        identb = const.tile([P, P], BF16, name="identb")
+        make_identity(nc, identb[:])
+
+        mk = const.tile([P, B * N], BF16, name="mk")
+        nc.sync.dma_start(out=mk[:], in_=dmask.rearrange("b o m -> (b o m)").partition_broadcast(P))
+
+        a_tiles = {}
+
+        def load_adj(u):
+            b, nt = u // NT, u % NT
+            a_t = a_pool.tile([P, N * R], BF16, name="a_t", tag="a_t")
+            nc.sync.dma_start(out=a_t[:], in_=adj[b, nt * P:(nt + 1) * P].rearrange("n m r -> n (m r)"))
+            a_tiles[u] = a_t
+
+        w_tiles = {}
+
+        def load_w(r):
+            wr = w_pool.tile([P, 4, H], BF16, name="wraw", tag="wraw")
+            nc.sync.dma_start(
+                out=wr[:].rearrange("p (u e) f -> p u (e f)", u=2),
+                in_=W[r].rearrange("(u p e) f -> p u (e f)", u=2, e=2),
+            )
+            w_tiles[r] = wr
+
+        x_tiles = []
+
+        def load_x(b):
+            xr = w_pool.tile([P, 4, H], BF16, name="xraw", tag="wraw")
+            nc.sync.dma_start(
+                out=xr[:].rearrange("p (a c) k -> p a (c k)", a=2),
+                in_=x[b].rearrange("(a p c) k -> p a (c k)", a=2, c=2),
+            )
+            x_tiles.append(xr)
+
+        load_x(0)
+        load_w(0)
+        load_x(1)
+        load_adj(0)
+
+        negs = []
+        for b in range(B):
+            mb = mk[:, b * N:(b + 1) * N]
+            mpair = mb.rearrange("p (mp c) -> p mp c", c=2)
+            n_e = const.tile([P, 1024], BF16, name="neg_e%d" % b)
+            n_x = const.tile([P, 1024], BF16, name="neg_x%d" % b)
+            n_o = const.tile([P, 1024], BF16, name="neg_o%d" % b)
+            jobs = (
+                (n_e[:].rearrange("p (mp q) -> p mp q", q=4), mpair[:, :, 0:1].to_broadcast([P, 256, 4])),
+                (n_x[:].rearrange("p (m q) -> p m q", q=2), mb.unsqueeze(2).to_broadcast([P, N, 2])),
+                (n_o[:].rearrange("p (mp q) -> p mp q", q=4), mpair[:, :, 1:2].to_broadcast([P, 256, 4])),
+            )
+            for q, (dst, src) in enumerate(jobs):
+                if b == 0 and q == 0:
+                    nc.scalar.activation(out=dst, in_=src, func=AF.Copy, scale=-BIG, bias=BIG)
+                elif b == 0:
+                    nc.vector.tensor_scalar(out=dst, in0=src, scalar1=-BIG, scalar2=BIG,
+                                            op0=ALU.mult, op1=ALU.add)
+                else:
+                    nc.gpsimd.tensor_scalar(out=dst, in0=src, scalar1=-BIG, scalar2=BIG,
+                                            op0=ALU.mult, op1=ALU.add)
+            negs.append((n_e, n_x, n_o))
+
+        xq, xs = [], []
+
+        def prep_x(b):
+            xw = x_tiles[b][:].rearrange("p s k -> p (s k)").bitcast(F32)
+            gx = gw_pool.tile([P, H, 4], BF16, name="gx", tag="gw", align_bytes=64)
+            gxw = gx[:].rearrange("p f t -> p (f t)").bitcast(F32)
+            for q in range(2):
+                xt = ps_t.tile([P, 4, P], F32, name="xt", tag="tp")
+                for tl in range(2):
+                    t = 2 * q + tl
+                    blk = (t % 2) * 2 + t // 2
+                    for u in range(2):
+                        c0 = blk * 256 + u * P
+                        nc.tensor.transpose(xt[:, tl * 2 + u, :], xw[:, c0:c0 + P], ident32[:])
+                nc.scalar.copy(
+                    out=gxw[:, q * 512:(q + 1) * 512].rearrange("p (t c u) -> p t c u", t=2, u=2),
+                    in_=xt[:].rearrange("p (t u) c -> p t c u", t=2))
+            xq_b = const.tile([P, N], U32, name="xq%d" % b, align_bytes=64)
+            xs_b = const.tile([P, N], U8, name="xs%d" % b, align_bytes=64)
+            nc.vector.quantize_mx(out=xq_b[:].bitcast(FP8X4), scales=xs_b[:],
+                                  in_=gx[:].rearrange("p f t -> p (f t)"))
+            xq.append(xq_b)
+            xs.append(xs_b)
+
+        hq, hs = {}, {}
+        wq_tiles, gh_tiles, hp_tiles = {}, {}, {}
+        lp_tiles, mn_tiles, ss_tiles, rs_tiles = {}, {}, {}, {}
+        e_tiles, at_tiles, tp_tiles, ga_tiles = {}, {}, {}, {}
+        aq_tiles, as_tiles, acc_tiles = {}, {}, {}
+        att_done = [set() for u in range(NU)]
+        h_done = set()
+        s2_seen = set()
+        s2_ready = []
+        s2_open = []
+        s2_count = [0 for u in range(NU)]
+
+        def w_regroup(r):
+            gw = gw_pool.tile([P, H, 4], BF16, name="gw", tag="gw", align_bytes=64)
+            eng = pick("regroup", r)
+            busy(eng, 1050.0 if eng == "V" else 2050.0)
+            eng_copy = nc.vector.tensor_copy if eng == "V" else nc.scalar.copy
+            eng_copy(
+                out=gw[:].rearrange("p (c i) t -> p c t i", i=4),
+                in_=w_tiles[r][:].rearrange("p t (c i) -> p c t i", i=4))
+            wq_tiles[r] = [gw]
+
+        def w_quant(r):
+            gw = wq_tiles[r][0]
+            wq = wq_pool.tile([P, H], U32, name="wq", tag="wq", align_bytes=64)
+            ws = wq_pool.tile([P, H], U8, name="ws", tag="ws", align_bytes=64)
+            busy("V", 540.0)
+            nc.vector.quantize_mx(out=wq[:].bitcast(FP8X4), scales=ws[:],
+                                  in_=gw[:].rearrange("p f t -> p (f t)"))
+            wq_tiles[r] = [wq, ws]
+
+        def h_mm(g):
+            r, b, c = g // 8, (g % 8) // 4, g % 4
+            wq, ws = wq_tiles[r]
+            hp = ps_h.tile([P, 4, P], F32, name="hp", tag="hp")
+            for t in range(4):
+                nc.tensor.matmul_mx(
+                    out=hp[:, t, :],
+                    lhsT=xq[b][:, t * P:(t + 1) * P].bitcast(FP8X4),
+                    lhsT_scale=xs[b][:, t * P:(t + 1) * P],
+                    rhs=wq[:, c * P:(c + 1) * P].bitcast(FP8X4),
+                    rhs_scale=ws[:, c * P:(c + 1) * P],
+                    start=True, stop=True)
+            hp_tiles[g] = hp
+
+        def h_ev(g):
+            r, b, c = g // 8, (g % 8) // 4, g % 4
+            if c == 0:
+                gh_tiles[(b, r)] = gh_pool.tile([P, 4 * H], BF16, name="gh", tag="gh", align_bytes=64)
+            gh = gh_tiles[(b, r)]
+            eng = pick("hev", g)
+            busy(eng, 512.0)
+            eng_copy = nc.vector.tensor_copy if eng == "V" else nc.scalar.copy
+            eng_copy(
+                out=gh[:, c * 512:(c + 1) * 512].rearrange("p (f t) -> p f t", t=4),
+                in_=hp_tiles[g][:].rearrange("p t f -> p f t"))
+
+        def h_quant(b, r):
+            hq_t = const.tile([P, H], U32, name="hq%d_%d" % (b, r), align_bytes=64)
+            hs_t = const.tile([P, H], U8, name="hs%d_%d" % (b, r), align_bytes=64)
+            busy("V", 540.0)
+            nc.vector.quantize_mx(out=hq_t[:].bitcast(FP8X4), scales=hs_t[:], in_=gh_tiles[(b, r)][:])
+            hq[(b, r)] = hq_t
+            hs[(b, r)] = hs_t
+            h_done.add((b, r))
+
+        def front_pieces(u):
+            b = u // NT
+            n_e, n_x, n_o = negs[b]
+            box = {}
+
+            def m1():
+                box["av"] = a_tiles[u][:].rearrange("p (mp g) -> p mp g", g=20)
+                lp = l_pool.tile([P, LPW], BF16, name="lp", tag="lp")
+                lp_tiles[u] = lp
+                busy("V", 1024.0)
+                nc.vector.tensor_tensor(
+                    out=lp[:, 0:2048].rearrange("p (j mp q) -> p j mp q", j=2, q=4),
+                    in0=n_e[:].rearrange("p (mp q) -> p mp q", q=4).unsqueeze(1).to_broadcast([P, 2, 256, 4]),
+                    in1=box["av"][:, :, 0:8].rearrange("p mp (j q) -> p j mp q", j=2),
+                    op=ALU.subtract)
+
+            def m2():
+                busy("V", 512.0)
+                nc.vector.tensor_tensor(
+                    out=lp_tiles[u][:, 2048:3072].rearrange("p (mp q) -> p mp q", q=4),
+                    in0=n_x[:].rearrange("p (mp q) -> p mp q", q=4),
+                    in1=box["av"][:, :, 8:12],
+                    op=ALU.subtract)
+
+            def m3():
+                busy("V", 1024.0)
+                nc.vector.tensor_tensor(
+                    out=lp_tiles[u][:, 3072:5120].rearrange("p (j mp q) -> p j mp q", j=2, q=4),
+                    in0=n_o[:].rearrange("p (mp q) -> p mp q", q=4).unsqueeze(1).to_broadcast([P, 2, 256, 4]),
+                    in1=box["av"][:, :, 12:20].rearrange("p mp (j q) -> p j mp q", j=2),
+                    op=ALU.subtract)
+
+            def level(w):
+                def go():
+                    if w == 512:
+                        box["tr"] = t_pool.tile([P, 5120], BF16, name="tr", tag="tr")
+                        box["src"] = lp_tiles[u][:, 0:5120].rearrange("p (j x) -> p j x", j=5)
+                        box["off"] = 0
+                    off = box["off"]
+                    dst = box["tr"][:, off:off + 5 * w].rearrange("p (j x) -> p j x", j=5)
+                    busy("V", 2.5 * w)
+                    nc.vector.tensor_tensor(out=dst, in0=box["src"][:, :, 0:w], in1=box["src"][:, :, w:2 * w],
+                                            op=ALU.min)
+                    box["src"] = dst
+                    box["last"] = off
+                    box["off"] = off + 5 * w
+                return go
+
+            def fin():
+                last = box["last"]
+                mn = st_pool.tile([P, R], F32, name="mn", tag="mn")
+                busy("V", 10.0)
+                nc.vector.tensor_tensor(out=mn[:], in0=box["tr"][:, last:last + R],
+                                        in1=box["tr"][:, last + R:last + 2 * R], op=ALU.min)
+                mn_tiles[u] = mn
+                ss_tiles[u] = st_pool.tile([P, R], F32, name="ss", tag="ss")
+                rs_tiles[u] = st_pool.tile([P, R], F32, name="rs", tag="rs")
+
+            return [m1, m2, m3] + [level(w) for w in (512, 256, 128, 64, 32, 16, 8, 4)] + [fin]
+
+        def exp_pair(i):
+            u, rp = i // 5, i % 5
+            e2 = e_pool.tile([P, 2, N], F32, name="e2", tag="e2")
+            lp = lp_tiles[u]
+            for rr in range(2):
+                r = 2 * rp + rr
+                base = plane_offset(r)
+                step = plane_offset(r + R) - base
+                view = lp[:, base:base + 2 * step].rearrange("p (s x) -> p s x", s=2)[:, :, 0:1024:4]
+                busy("A", 512.0)
+                nc.scalar.activation(
+                    out=e2[:, rr, :].rearrange("p (s mp) -> p s mp", s=2), in_=view, func=AF.Exp,
+                    bias=mn_tiles[u][:, r:r + 1], scale=-1.0, accum_out=ss_tiles[u][:, r:r + 1])
+            e_tiles[i] = e2
+
+        def recip(i):
+            u, rp = i // 5, i % 5
+            busy("V", 36.0)
+            nc.vector.reciprocal(out=rs_tiles[u][:, 2 * rp:2 * rp + 2], in_=ss_tiles[u][:, 2 * rp:2 * rp + 2])
+
+        def norm_one(i, rr):
+            u, rp = i // 5, i % 5
+            e2 = e_tiles[i]
+            rs = rs_tiles[u]
+            if rr == 0:
+                at_tiles[i] = at_pool.tile([P, 2, N], BF16, name="at2", tag="at2")
+            at2 = at_tiles[i]
+            r = 2 * rp + rr
+            eng = "A" if (rr == 1 and hstate["ev"] >= 80 and i < 5 * (NU - 1) - 2) else "V"
+            if eng == "A":
+                nc.scalar.activation(out=at2[:, rr, :], in_=e2[:, rr, :], func=AF.Copy, scale=rs[:, r:r + 1])
+            else:
+                nc.vector.tensor_scalar(out=at2[:, rr, :], in0=e2[:, rr, :], scalar1=rs[:, r:r + 1],
+                                        scalar2=None, op0=ALU.mult)
+
+        def transposes(i):
+            at2 = at_tiles[i]
+            tp = ps_t.tile([P, 8, P], BF16, name="tp", tag="tp")
+            for rr in range(2):
+                for t in range(4):
+                    nc.tensor.transpose(tp[:, rr * 4 + t, :], at2[:, rr, t * P:(t + 1) * P], identb[:])
+            tp_tiles[i] = tp
+
+        def att_ev(i):
+            ga = ga_pool.tile([P, 1024], BF16, name="ga", tag="ga", align_bytes=64)
+            eng = pick("aev", i)
+            busy(eng, 1024.0)
+            eng_copy = nc.vector.tensor_copy if eng == "V" else nc.scalar.copy
+            eng_copy(out=ga[:].rearrange("p (r n t) -> p r n t", r=2, t=4),
+                     in_=tp_tiles[i][:].rearrange("p (r t) n -> p r n t", r=2))
+            ga_tiles[i] = ga
+
+        def att_quant(i):
+            u, rp = i // 5, i % 5
+            if rp == 0:
+                aq_tiles[u] = aq_pool.tile([P, R * P], U32, name="aq", tag="aq", align_bytes=64)
+                as_tiles[u] = aq_pool.tile([P, R * P], U8, name="asc", tag="asc", align_bytes=64)
+            busy("V", 270.0)
+            nc.vector.quantize_mx(out=aq_tiles[u][:, rp * 256:(rp + 1) * 256].bitcast(FP8X4),
+                                  scales=as_tiles[u][:, rp * 256:(rp + 1) * 256], in_=ga_tiles[i][:])
+            att_done[u].add(2 * rp)
+            att_done[u].add(2 * rp + 1)
+
+        def s2_mm(u, r):
+            b = u // NT
+            gp = ps_g.tile([P, H], F32, name="gp", tag="gp")
+            nc.tensor.matmul_mx(
+                out=gp[:],
+                lhsT=aq_tiles[u][:, r * P:(r + 1) * P].bitcast(FP8X4),
+                lhsT_scale=as_tiles[u][:, r * P:(r + 1) * P],
+                rhs=hq[(b, r)][:].bitcast(FP8X4),
+                rhs_scale=hs[(b, r)][:],
+                start=True, stop=True)
+            s2_open.append((u, r, gp))
+
+        def s2_ev():
+            u, r, gp = s2_open.pop(0)
+            b, nt = u // NT, u % NT
+            if s2_count[u] == 0:
+                acc_tiles[u] = acc_pool.tile([P, H], F32, name="acc", tag="acc")
+                busy("A", 512.0)
+                nc.scalar.activation(out=acc_tiles[u][:], in_=gp[:], func=AF.Relu)
+            else:
+                acc = acc_tiles[u]
+                busy("V", 512.0)
+                nc.vector.scalar_tensor_tensor(out=acc[:], in0=gp[:], scalar=0.0, in1=acc[:],
+                                               op0=ALU.max, op1=ALU.add)
+            s2_count[u] += 1
+            if s2_count[u] == R:
+                nc.sync.dma_start(out=out[b, nt * P:(nt + 1) * P, :], in_=acc_tiles[u][:])
+
+        def s2_collect():
+            for u in range(NU):
+                for r in range(R):
+                    if (u, r) not in s2_seen and r in att_done[u] and (u // NT, r) in h_done:
+                        s2_seen.add((u, r))
+                        s2_ready.append((u, r))
+
+        def s2_drain(late):
+            keep = []
+            fresh = set()
+            while s2_open:
+                u = s2_open[0][0]
+                if not late and u in fresh:
+                    keep.append(s2_open.pop(0))
+                    continue
+                if s2_count[u] == 0:
+                    fresh.add(u)
+                s2_ev()
+            s2_open.extend(keep)
+
+        def s2_issue(limit):
+            s2_collect()
+            n = 0
+            while s2_ready and n < limit:
+                if len(s2_open) == G_BANKS:
+                    s2_ev()
+                u, r = s2_ready.pop(0)
+                s2_mm(u, r)
+                n += 1
+
+        hstate = {"mm": 0, "ev": 0, "wr": 0, "wq": 0}
+        hq_wait = []
+        fq = []
+
+        def front_tick(n=1):
+            for q in range(n):
+                if fq:
+                    fq.pop(0)()
+
+        def h_fill():
+            while hstate["mm"] < 80 and hstate["mm"] < hstate["ev"] + H_BANKS and hstate["mm"] // 8 < hstate["wq"]:
+                h_mm(hstate["mm"])
+                hstate["mm"] += 1
+
+        def h_vector_tick():
+            if hq_wait and hq_wait[0][2] <= hstate["ev"]:
+                b, r, when = hq_wait.pop(0)
+                h_quant(b, r)
+            elif hstate["wq"] < hstate["wr"]:
+                w_quant(hstate["wq"])
+                hstate["wq"] += 1
+                h_fill()
+            elif hstate["wr"] < R and hstate["wr"] * 8 < hstate["ev"] + W_AHEAD:
+                r = hstate["wr"]
+                w_regroup(r)
+                if r + 2 < R:
+                    load_w(r + 2)
+                hstate["wr"] += 1
+
+        def h_banks(n):
+            for q in range(n):
+                g = hstate["ev"]
+                if g >= 80 or g >= hstate["mm"]:
+                    return
+                h_ev(g)
+                hstate["ev"] += 1
+                h_fill()
+                if g % 4 == 3:
+                    hq_wait.append(((g % 8) // 4, g // 8, min(g + 2, 80)))
+
+        def s2_one():
+            if s2_open:
+                s2_ev()
+
+        prep_x(0)
+        h_vector_tick()
+        load_w(1)
+        h_vector_tick()
+        prep_x(1)
+        h_fill()
+        load_adj(1)
+        fq.extend(front_pieces(0))
+        for q in range(len(HEAD_BANKS)):
+            h_banks(HEAD_BANKS[q])
+            front_tick()
+            h_vector_tick()
+        NPAIR = 5 * NU
+        for j in range(-E_AHEAD, NPAIR + 3):
+            un = (j + E_AHEAD) // 5 + 1
+            if (j + E_AHEAD) % 5 == 0 and 0 < un < NU:
+                fq.extend(front_pieces(un))
+                if un + 1 < NU:
+                    load_adj(un + 1)
+            nf = FRONT_TICKS[(j + E_AHEAD) % 5]
+            if 0 <= j + 1 < NPAIR:
+                recip(j + 1)
+            front_tick(nf[0])
+            s2_one()
+            if 0 <= j < NPAIR:
+                att_ev(j)
+            if 0 <= j - 1 < NPAIR:
+                att_quant(j - 1)
+            front_tick(nf[1])
+            if 0 <= j + 1 < NPAIR:
+                norm_one(j + 1, 0)
+            s2_one()
+            front_tick(nf[2])
+            if 0 <= j + 1 < NPAIR:
+                norm_one(j + 1, 1)
+                transposes(j + 1)
+            s2_one()
+            s2_issue(S2_PER_STEP)
+            if 0 <= j + E_AHEAD < NPAIR:
+                exp_pair(j + E_AHEAD)
+            front_tick(nf[3])
+            h_vector_tick()
+            h_banks(h_rate(j))
+            front_tick(nf[4])
+            h_vector_tick()
+            front_tick(nf[5])
+        while hq_wait:
+            h_vector_tick()
+        s2_issue(100)
+        while s2_open:
+            s2_ev()

@@ -25,7 +25,7 @@ FIXED = {"V": 36.0, "A": 50.0}
 G_BANKS = 3
 S2_PER_STEP = 4
 HEAD_BANKS = (2, 2, 2, 2, 2, 2, 2, 2, 2, 2, 2, 2)
-FRONT_TICKS = ((1, 0, 1, 0, 0, 0), (0, 1, 0, 0, 0, 0), (0, 0, 1, 0, 0, 0), (1, 0, 0, 1, 0, 0), (1, 1, 1, 1, 1, 1))
+FRONT_TICKS = ((1, 0, 1, 0, 0, 0), (0, 1, 0, 0, 0, 0), (0, 0, 1, 0, 0, 0), (1, 0, 0, 1, 0, 0), (1, 0, 1, 0, 1, 1))
 
 
 def plane_offset(t):
@@ -80,8 +80,11 @@ def tile_rgat_pa_kernel(tc, adj, x, dmask, W, out):
         identb = const.tile([P, P], BF16, name="identb")
         make_identity(nc, identb[:])
 
+        zrow = const.tile([P, B * N], BF16, name="zrow")
+        nc.vector.memset(zrow[:], 0.0)
+        ones = const.tile([P, P], BF16, name="ones")
+        nc.vector.memset(ones[:], 1.0)
         mk = const.tile([P, B * N], BF16, name="mk")
-        nc.sync.dma_start(out=mk[:], in_=dmask.rearrange("b o m -> (b o m)").partition_broadcast(P))
 
         a_tiles = {}
 
@@ -113,8 +116,13 @@ def tile_rgat_pa_kernel(tc, adj, x, dmask, W, out):
 
         load_x(0)
         load_w(0)
+        nc.sync.dma_start(out=zrow[0:1, :], in_=dmask.rearrange("b o m -> o (b m)"))
         load_x(1)
         load_adj(0)
+        for b in range(B):
+            mkp = ps_g.tile([P, N], F32, name="mkp", tag="gp")
+            nc.tensor.matmul(out=mkp[:], lhsT=ones[:], rhs=zrow[:, b * N:(b + 1) * N], start=True, stop=True)
+            nc.scalar.copy(out=mk[:, b * N:(b + 1) * N], in_=mkp[:])
 
         negs = []
         for b in range(B):
@@ -129,7 +137,7 @@ def tile_rgat_pa_kernel(tc, adj, x, dmask, W, out):
                 (n_o[:].rearrange("p (mp q) -> p mp q", q=4), mpair[:, :, 1:2].to_broadcast([P, 256, 4])),
             )
             for q, (dst, src) in enumerate(jobs):
-                if b == 0 and q == 0:
+                if b == 0:
                     nc.scalar.activation(out=dst, in_=src, func=AF.Copy, scale=-BIG, bias=BIG)
                 elif b == 0:
                     nc.vector.tensor_scalar(out=dst, in0=src, scalar1=-BIG, scalar2=BIG,
@@ -287,7 +295,15 @@ def tile_rgat_pa_kernel(tc, adj, x, dmask, W, out):
                 ss_tiles[u] = st_pool.tile([P, R], F32, name="ss", tag="ss")
                 rs_tiles[u] = st_pool.tile([P, R], F32, name="rs", tag="rs")
 
-            return [m1, m2, m3] + [level(w) for w in (512, 256, 128, 64, 32, 16, 8, 4)] + [fin]
+            def tail():
+                off = box["off"]
+                dst = box["tr"][:, off:off + 20].rearrange("p (j q) -> p j q", j=5)
+                busy("V", 160.0)
+                nc.vector.tensor_reduce(out=dst, in_=box["src"].rearrange("p j (mp q) -> p j q mp", q=4),
+                                        axis=mybir.AxisListType.X, op=ALU.min)
+                box["last"] = off
+
+            return [m1, m2, m3] + [level(w) for w in (512, 256, 128, 64, 32)] + [tail, fin]
 
         def exp_pair(i):
             u, rp = i // 5, i % 5
@@ -317,7 +333,7 @@ def tile_rgat_pa_kernel(tc, adj, x, dmask, W, out):
                 at_tiles[i] = at_pool.tile([P, 2, N], BF16, name="at2", tag="at2")
             at2 = at_tiles[i]
             r = 2 * rp + rr
-            eng = "A" if (rr == 1 and hstate["ev"] >= 80 and i < 5 * (NU - 1) - 2) else "V"
+            eng = "V"
             if eng == "A":
                 nc.scalar.activation(out=at2[:, rr, :], in_=e2[:, rr, :], func=AF.Copy, scale=rs[:, r:r + 1])
             else:

@@ -77,8 +77,6 @@ def tile_rgat_pa_kernel(tc, adj, x, dmask, W, out):
         nc.scalar.activation(out=warm[:], in_=warm[:], func=AF.Exp)
         ident32 = const.tile([P, P], F32, name="ident32")
         make_identity(nc, ident32[:])
-        identb = const.tile([P, P], BF16, name="identb")
-        make_identity(nc, identb[:])
 
         zrow = const.tile([P, B * N], BF16, name="zrow")
         nc.vector.memset(zrow[:], 0.0)
@@ -157,9 +155,8 @@ def tile_rgat_pa_kernel(tc, adj, x, dmask, W, out):
                 xt = ps_t.tile([P, 4, P], F32, name="xt", tag="tp")
                 for tl in range(2):
                     t = 2 * q + tl
-                    blk = (t % 2) * 2 + t // 2
                     for u in range(2):
-                        c0 = blk * 256 + u * P
+                        c0 = t * 256 + u * P
                         nc.tensor.transpose(xt[:, tl * 2 + u, :], xw[:, c0:c0 + P], ident32[:])
                 nc.scalar.copy(
                     out=gxw[:, q * 512:(q + 1) * 512].rearrange("p (t c u) -> p t c u", t=2, u=2),
@@ -313,10 +310,10 @@ def tile_rgat_pa_kernel(tc, adj, x, dmask, W, out):
                 r = 2 * rp + rr
                 base = plane_offset(r)
                 step = plane_offset(r + R) - base
-                view = lp[:, base:base + 2 * step].rearrange("p (s x) -> p s x", s=2)[:, :, 0:1024:4]
+                view = lp[:, base:base + 2 * step].rearrange("p (s x) -> p x s", s=2)[:, 0:1024:4, :]
                 busy("A", 512.0)
                 nc.scalar.activation(
-                    out=e2[:, rr, :].rearrange("p (s mp) -> p s mp", s=2), in_=view, func=AF.Exp,
+                    out=e2[:, rr, :].rearrange("p (mp s) -> p mp s", s=2), in_=view, func=AF.Exp,
                     bias=mn_tiles[u][:, r:r + 1], scale=-1.0, accum_out=ss_tiles[u][:, r:r + 1])
             e_tiles[i] = e2
 
@@ -342,10 +339,11 @@ def tile_rgat_pa_kernel(tc, adj, x, dmask, W, out):
 
         def transposes(i):
             at2 = at_tiles[i]
-            tp = ps_t.tile([P, 8, P], BF16, name="tp", tag="tp")
+            tp = ps_t.tile([P, 4, P], F32, name="tp", tag="tp")
             for rr in range(2):
-                for t in range(4):
-                    nc.tensor.transpose(tp[:, rr * 4 + t, :], at2[:, rr, t * P:(t + 1) * P], identb[:])
+                words = at2[:, rr, :].bitcast(F32)
+                for u in range(2):
+                    nc.tensor.transpose(tp[:, rr * 2 + u, :], words[:, u * P:(u + 1) * P], ident32[:])
             tp_tiles[i] = tp
 
         def att_ev(i):
@@ -353,8 +351,8 @@ def tile_rgat_pa_kernel(tc, adj, x, dmask, W, out):
             eng = pick("aev", i)
             busy(eng, 1024.0)
             eng_copy = nc.vector.tensor_copy if eng == "V" else nc.scalar.copy
-            eng_copy(out=ga[:].rearrange("p (r n t) -> p r n t", r=2, t=4),
-                     in_=tp_tiles[i][:].rearrange("p (r t) n -> p r n t", r=2))
+            eng_copy(out=ga[:].bitcast(F32).rearrange("p (r n u) -> p r n u", r=2, u=2),
+                     in_=tp_tiles[i][:].rearrange("p (r u) n -> p r n u", r=2))
             ga_tiles[i] = ga
 
         def att_quant(i):

@@ -21,27 +21,17 @@ LPW = 7168
 H_BANKS = 3
 E_AHEAD = 3
 W_AHEAD = 12
-FIXED = {"V": 36.0, "A": 50.0}
 G_BANKS = 3
+W_SCALAR = ()
+NS_FROM = 10
 S2_PER_STEP = 4
+H_RATE = 3
 HEAD_BANKS = (2, 2, 2, 2, 2, 2, 2, 2, 2, 2, 2, 2)
 FRONT_TICKS = ((1, 0, 1, 0, 0, 0), (0, 1, 0, 0, 0, 0), (0, 0, 1, 0, 0, 0), (1, 0, 0, 1, 0, 0), (1, 0, 1, 0, 1, 1))
 
 
 def plane_offset(t):
     return (t // 4) * 1024 + t % 4
-
-
-def on_vector(kind, idx):
-    if kind == "regroup":
-        return True
-    if kind == "norm":
-        return not (idx >= 50 and idx % 2 == 1)
-    return False
-
-
-def h_rate(j):
-    return 3
 
 
 def tile_rgat_pa_kernel(tc, adj, x, dmask, W, out):
@@ -65,13 +55,6 @@ def tile_rgat_pa_kernel(tc, adj, x, dmask, W, out):
         ps_g = ctx.enter_context(tc.psum_pool(name="ps_g", bufs=G_BANKS))
         ps_t = ctx.enter_context(tc.psum_pool(name="ps_t", bufs=2))
 
-        load = {"V": 0.0, "A": 0.0}
-
-        def busy(eng, cycles):
-            load[eng] += cycles + FIXED[eng]
-
-        def pick(kind, idx):
-            return "V" if on_vector(kind, idx) else "A"
         warm = const.tile([P, 1], F32, name="warm")
         nc.vector.memset(warm[:], 0.0)
         nc.scalar.activation(out=warm[:], in_=warm[:], func=AF.Exp)
@@ -82,7 +65,6 @@ def tile_rgat_pa_kernel(tc, adj, x, dmask, W, out):
         nc.vector.memset(zrow[:], 0.0)
         ones = const.tile([P, P], BF16, name="ones")
         nc.vector.memset(ones[:], 1.0)
-        mk = const.tile([P, B * N], BF16, name="mk")
 
         a_tiles = {}
 
@@ -117,34 +99,25 @@ def tile_rgat_pa_kernel(tc, adj, x, dmask, W, out):
         nc.sync.dma_start(out=zrow[0:1, :], in_=dmask.rearrange("b o m -> o (b m)"))
         load_x(1)
         load_adj(0)
-        for b in range(B):
+        negs = []
+
+        def make_masks(b):
             mkp = ps_g.tile([P, N], F32, name="mkp", tag="gp")
             nc.tensor.matmul(out=mkp[:], lhsT=ones[:], rhs=zrow[:, b * N:(b + 1) * N], start=True, stop=True)
-            nc.scalar.copy(out=mk[:, b * N:(b + 1) * N], in_=mkp[:])
-
-        negs = []
-        for b in range(B):
-            mb = mk[:, b * N:(b + 1) * N]
-            mpair = mb.rearrange("p (mp c) -> p mp c", c=2)
             n_e = const.tile([P, 1024], BF16, name="neg_e%d" % b)
             n_x = const.tile([P, 1024], BF16, name="neg_x%d" % b)
             n_o = const.tile([P, 1024], BF16, name="neg_o%d" % b)
-            jobs = (
-                (n_e[:].rearrange("p (mp q) -> p mp q", q=4), mpair[:, :, 0:1].to_broadcast([P, 256, 4])),
-                (n_x[:].rearrange("p (m q) -> p m q", q=2), mb.unsqueeze(2).to_broadcast([P, N, 2])),
-                (n_o[:].rearrange("p (mp q) -> p mp q", q=4), mpair[:, :, 1:2].to_broadcast([P, 256, 4])),
-            )
-            for q, (dst, src) in enumerate(jobs):
-                if b == 0:
-                    nc.scalar.activation(out=dst, in_=src, func=AF.Copy, scale=-BIG, bias=BIG)
-                elif b == 0:
-                    nc.vector.tensor_scalar(out=dst, in0=src, scalar1=-BIG, scalar2=BIG,
-                                            op0=ALU.mult, op1=ALU.add)
-                else:
-                    nc.gpsimd.tensor_scalar(out=dst, in0=src, scalar1=-BIG, scalar2=BIG,
-                                            op0=ALU.mult, op1=ALU.add)
+            nc.scalar.activation(out=n_x[:].rearrange("p (m q) -> p m q", q=2),
+                                 in_=mkp[:].unsqueeze(2).to_broadcast([P, N, 2]),
+                                 func=AF.Copy, scale=-BIG, bias=BIG)
+            both = n_x[:].rearrange("p (mp c q) -> p mp c q", c=2, q=2)
+            for c, dst in ((0, n_e), (1, n_o)):
+                nc.vector.tensor_copy(out=dst[:].rearrange("p (mp d q) -> p mp d q", d=2, q=2),
+                                      in_=both[:, :, c:c + 1, :].to_broadcast([P, 256, 2, 2]))
             negs.append((n_e, n_x, n_o))
 
+        ss = const.tile([P, NU * R], F32, name="ss")
+        rs = const.tile([P, NU * R], F32, name="rs")
         xq, xs = [], []
 
         def prep_x(b):
@@ -170,7 +143,7 @@ def tile_rgat_pa_kernel(tc, adj, x, dmask, W, out):
 
         hq, hs = {}, {}
         wq_tiles, gh_tiles, hp_tiles = {}, {}, {}
-        lp_tiles, mn_tiles, ss_tiles, rs_tiles = {}, {}, {}, {}
+        lp_tiles, mn_tiles = {}, {}
         e_tiles, at_tiles, tp_tiles, ga_tiles = {}, {}, {}, {}
         aq_tiles, as_tiles, acc_tiles = {}, {}, {}
         att_done = [set() for u in range(NU)]
@@ -182,10 +155,8 @@ def tile_rgat_pa_kernel(tc, adj, x, dmask, W, out):
 
         def w_regroup(r):
             gw = gw_pool.tile([P, H, 4], BF16, name="gw", tag="gw", align_bytes=64)
-            eng = pick("regroup", r)
-            busy(eng, 1050.0 if eng == "V" else 2050.0)
-            eng_copy = nc.vector.tensor_copy if eng == "V" else nc.scalar.copy
-            eng_copy(
+            copy = nc.vector.tensor_copy if r not in W_SCALAR else nc.scalar.copy
+            copy(
                 out=gw[:].rearrange("p (c i) t -> p c t i", i=4),
                 in_=w_tiles[r][:].rearrange("p t (c i) -> p c t i", i=4))
             wq_tiles[r] = [gw]
@@ -194,7 +165,6 @@ def tile_rgat_pa_kernel(tc, adj, x, dmask, W, out):
             gw = wq_tiles[r][0]
             wq = wq_pool.tile([P, H], U32, name="wq", tag="wq", align_bytes=64)
             ws = wq_pool.tile([P, H], U8, name="ws", tag="ws", align_bytes=64)
-            busy("V", 540.0)
             nc.vector.quantize_mx(out=wq[:].bitcast(FP8X4), scales=ws[:],
                                   in_=gw[:].rearrange("p f t -> p (f t)"))
             wq_tiles[r] = [wq, ws]
@@ -218,17 +188,13 @@ def tile_rgat_pa_kernel(tc, adj, x, dmask, W, out):
             if c == 0:
                 gh_tiles[(b, r)] = gh_pool.tile([P, 4 * H], BF16, name="gh", tag="gh", align_bytes=64)
             gh = gh_tiles[(b, r)]
-            eng = pick("hev", g)
-            busy(eng, 512.0)
-            eng_copy = nc.vector.tensor_copy if eng == "V" else nc.scalar.copy
-            eng_copy(
+            nc.scalar.copy(
                 out=gh[:, c * 512:(c + 1) * 512].rearrange("p (f t) -> p f t", t=4),
                 in_=hp_tiles[g][:].rearrange("p t f -> p f t"))
 
         def h_quant(b, r):
             hq_t = const.tile([P, H], U32, name="hq%d_%d" % (b, r), align_bytes=64)
             hs_t = const.tile([P, H], U8, name="hs%d_%d" % (b, r), align_bytes=64)
-            busy("V", 540.0)
             nc.vector.quantize_mx(out=hq_t[:].bitcast(FP8X4), scales=hs_t[:], in_=gh_tiles[(b, r)][:])
             hq[(b, r)] = hq_t
             hs[(b, r)] = hs_t
@@ -243,7 +209,6 @@ def tile_rgat_pa_kernel(tc, adj, x, dmask, W, out):
                 box["av"] = a_tiles[u][:].rearrange("p (mp g) -> p mp g", g=20)
                 lp = l_pool.tile([P, LPW], BF16, name="lp", tag="lp")
                 lp_tiles[u] = lp
-                busy("V", 1024.0)
                 nc.vector.tensor_tensor(
                     out=lp[:, 0:2048].rearrange("p (j mp q) -> p j mp q", j=2, q=4),
                     in0=n_e[:].rearrange("p (mp q) -> p mp q", q=4).unsqueeze(1).to_broadcast([P, 2, 256, 4]),
@@ -251,7 +216,6 @@ def tile_rgat_pa_kernel(tc, adj, x, dmask, W, out):
                     op=ALU.subtract)
 
             def m2():
-                busy("V", 512.0)
                 nc.vector.tensor_tensor(
                     out=lp_tiles[u][:, 2048:3072].rearrange("p (mp q) -> p mp q", q=4),
                     in0=n_x[:].rearrange("p (mp q) -> p mp q", q=4),
@@ -259,7 +223,6 @@ def tile_rgat_pa_kernel(tc, adj, x, dmask, W, out):
                     op=ALU.subtract)
 
             def m3():
-                busy("V", 1024.0)
                 nc.vector.tensor_tensor(
                     out=lp_tiles[u][:, 3072:5120].rearrange("p (j mp q) -> p j mp q", j=2, q=4),
                     in0=n_o[:].rearrange("p (mp q) -> p mp q", q=4).unsqueeze(1).to_broadcast([P, 2, 256, 4]),
@@ -269,36 +232,24 @@ def tile_rgat_pa_kernel(tc, adj, x, dmask, W, out):
             def level(w):
                 def go():
                     if w == 512:
-                        box["tr"] = t_pool.tile([P, 5120], BF16, name="tr", tag="tr")
-                        box["src"] = lp_tiles[u][:, 0:5120].rearrange("p (j x) -> p j x", j=5)
-                        box["off"] = 0
-                    off = box["off"]
-                    dst = box["tr"][:, off:off + 5 * w].rearrange("p (j x) -> p j x", j=5)
-                    busy("V", 2.5 * w)
-                    nc.vector.tensor_tensor(out=dst, in0=box["src"][:, :, 0:w], in1=box["src"][:, :, w:2 * w],
+                        box["tr"] = t_pool.tile([P, 5, 512], BF16, name="tr", tag="tr")
+                        src = lp_tiles[u][:, 0:5120].rearrange("p (j x) -> p j x", j=5)
+                    else:
+                        src = box["tr"]
+                    nc.vector.tensor_tensor(out=box["tr"][:, :, 0:w], in0=src[:, :, 0:w], in1=src[:, :, w:2 * w],
                                             op=ALU.min)
-                    box["src"] = dst
-                    box["last"] = off
-                    box["off"] = off + 5 * w
                 return go
 
-            def fin():
-                last = box["last"]
-                mn = st_pool.tile([P, R], F32, name="mn", tag="mn")
-                busy("V", 10.0)
-                nc.vector.tensor_tensor(out=mn[:], in0=box["tr"][:, last:last + R],
-                                        in1=box["tr"][:, last + R:last + 2 * R], op=ALU.min)
-                mn_tiles[u] = mn
-                ss_tiles[u] = st_pool.tile([P, R], F32, name="ss", tag="ss")
-                rs_tiles[u] = st_pool.tile([P, R], F32, name="rs", tag="rs")
-
             def tail():
-                off = box["off"]
-                dst = box["tr"][:, off:off + 20].rearrange("p (j q) -> p j q", j=5)
-                busy("V", 160.0)
-                nc.vector.tensor_reduce(out=dst, in_=box["src"].rearrange("p j (mp q) -> p j q mp", q=4),
+                nc.vector.tensor_reduce(out=box["tr"][:, 0, 64:84].rearrange("p (j q) -> p j q", j=5),
+                                        in_=box["tr"][:, :, 0:32].rearrange("p j (mp q) -> p j q mp", q=4),
                                         axis=mybir.AxisListType.X, op=ALU.min)
-                box["last"] = off
+
+            def fin():
+                mn = st_pool.tile([P, R], F32, name="mn", tag="mn")
+                nc.vector.tensor_tensor(out=mn[:], in0=box["tr"][:, 0, 64:64 + R],
+                                        in1=box["tr"][:, 0, 64 + R:64 + 2 * R], op=ALU.min)
+                mn_tiles[u] = mn
 
             return [m1, m2, m3] + [level(w) for w in (512, 256, 128, 64, 32)] + [tail, fin]
 
@@ -311,27 +262,22 @@ def tile_rgat_pa_kernel(tc, adj, x, dmask, W, out):
                 base = plane_offset(r)
                 step = plane_offset(r + R) - base
                 view = lp[:, base:base + 2 * step].rearrange("p (s x) -> p x s", s=2)[:, 0:1024:4, :]
-                busy("A", 512.0)
                 nc.scalar.activation(
                     out=e2[:, rr, :].rearrange("p (mp s) -> p mp s", s=2), in_=view, func=AF.Exp,
-                    bias=mn_tiles[u][:, r:r + 1], scale=-1.0, accum_out=ss_tiles[u][:, r:r + 1])
+                    bias=mn_tiles[u][:, r:r + 1], scale=-1.0, accum_out=ss[:, 2 * i + rr:2 * i + rr + 1])
             e_tiles[i] = e2
 
         def recip(i):
-            u, rp = i // 5, i % 5
-            busy("V", 36.0)
-            nc.vector.reciprocal(out=rs_tiles[u][:, 2 * rp:2 * rp + 2], in_=ss_tiles[u][:, 2 * rp:2 * rp + 2])
+            if i % 2 == 0:
+                nc.vector.reciprocal(out=rs[:, 2 * i:2 * i + 4], in_=ss[:, 2 * i:2 * i + 4])
 
         def norm_one(i, rr):
-            u, rp = i // 5, i % 5
             e2 = e_tiles[i]
-            rs = rs_tiles[u]
             if rr == 0:
                 at_tiles[i] = at_pool.tile([P, 2, N], BF16, name="at2", tag="at2")
             at2 = at_tiles[i]
-            r = 2 * rp + rr
-            eng = "V"
-            if eng == "A":
+            r = 2 * i + rr
+            if i >= NS_FROM and rr == 1:
                 nc.scalar.activation(out=at2[:, rr, :], in_=e2[:, rr, :], func=AF.Copy, scale=rs[:, r:r + 1])
             else:
                 nc.vector.tensor_scalar(out=at2[:, rr, :], in0=e2[:, rr, :], scalar1=rs[:, r:r + 1],
@@ -348,10 +294,7 @@ def tile_rgat_pa_kernel(tc, adj, x, dmask, W, out):
 
         def att_ev(i):
             ga = ga_pool.tile([P, 1024], BF16, name="ga", tag="ga", align_bytes=64)
-            eng = pick("aev", i)
-            busy(eng, 1024.0)
-            eng_copy = nc.vector.tensor_copy if eng == "V" else nc.scalar.copy
-            eng_copy(out=ga[:].bitcast(F32).rearrange("p (r n u) -> p r n u", r=2, u=2),
+            nc.scalar.copy(out=ga[:].bitcast(F32).rearrange("p (r n u) -> p r n u", r=2, u=2),
                      in_=tp_tiles[i][:].rearrange("p (r u) n -> p r n u", r=2))
             ga_tiles[i] = ga
 
@@ -360,7 +303,6 @@ def tile_rgat_pa_kernel(tc, adj, x, dmask, W, out):
             if rp == 0:
                 aq_tiles[u] = aq_pool.tile([P, R * P], U32, name="aq", tag="aq", align_bytes=64)
                 as_tiles[u] = aq_pool.tile([P, R * P], U8, name="asc", tag="asc", align_bytes=64)
-            busy("V", 270.0)
             nc.vector.quantize_mx(out=aq_tiles[u][:, rp * 256:(rp + 1) * 256].bitcast(FP8X4),
                                   scales=as_tiles[u][:, rp * 256:(rp + 1) * 256], in_=ga_tiles[i][:])
             att_done[u].add(2 * rp)
@@ -383,11 +325,9 @@ def tile_rgat_pa_kernel(tc, adj, x, dmask, W, out):
             b, nt = u // NT, u % NT
             if s2_count[u] == 0:
                 acc_tiles[u] = acc_pool.tile([P, H], F32, name="acc", tag="acc")
-                busy("A", 512.0)
                 nc.scalar.activation(out=acc_tiles[u][:], in_=gp[:], func=AF.Relu)
             else:
                 acc = acc_tiles[u]
-                busy("V", 512.0)
                 nc.vector.scalar_tensor_tensor(out=acc[:], in0=gp[:], scalar=0.0, in1=acc[:],
                                                op0=ALU.max, op1=ALU.add)
             s2_count[u] += 1
@@ -468,7 +408,9 @@ def tile_rgat_pa_kernel(tc, adj, x, dmask, W, out):
             if s2_open:
                 s2_ev()
 
+        make_masks(0)
         prep_x(0)
+        make_masks(1)
         h_vector_tick()
         load_w(1)
         h_vector_tick()
@@ -510,7 +452,7 @@ def tile_rgat_pa_kernel(tc, adj, x, dmask, W, out):
                 exp_pair(j + E_AHEAD)
             front_tick(nf[3])
             h_vector_tick()
-            h_banks(h_rate(j))
+            h_banks(H_RATE)
             front_tick(nf[4])
             h_vector_tick()
             front_tick(nf[5])

@@ -94,11 +94,11 @@ def tile_rgat_pa_kernel(tc, adj, x, dmask, W, out):
             )
             x_tiles.append(xr)
 
-        load_x(0)
         load_w(0)
+        load_x(0)
         nc.sync.dma_start(out=zrow[0:1, :], in_=dmask.rearrange("b o m -> o (b m)"))
-        load_x(1)
         load_adj(0)
+        load_x(1)
         negs = []
 
         def make_masks(b):
@@ -150,6 +150,7 @@ def tile_rgat_pa_kernel(tc, adj, x, dmask, W, out):
         h_done = set()
         s2_seen = set()
         s2_ready = []
+        sides = []
         s2_open = []
         s2_count = [0 for u in range(NU)]
 
@@ -277,7 +278,7 @@ def tile_rgat_pa_kernel(tc, adj, x, dmask, W, out):
                 at_tiles[i] = at_pool.tile([P, 2, N], BF16, name="at2", tag="at2")
             at2 = at_tiles[i]
             r = 2 * i + rr
-            if i >= NS_FROM and rr == 1:
+            if 2 <= i // 5 <= 6 and rr == 1:
                 nc.scalar.activation(out=at2[:, rr, :], in_=e2[:, rr, :], func=AF.Copy, scale=rs[:, r:r + 1])
             else:
                 nc.vector.tensor_scalar(out=at2[:, rr, :], in0=e2[:, rr, :], scalar1=rs[:, r:r + 1],
@@ -323,7 +324,14 @@ def tile_rgat_pa_kernel(tc, adj, x, dmask, W, out):
         def s2_ev():
             u, r, gp = s2_open.pop(0)
             b, nt = u // NT, u % NT
-            if s2_count[u] == 0:
+            if u == NU - 1 and s2_count[u] == 1:
+                side = acc_pool.tile([P, H], F32, name="acc", tag="acc")
+                sides.append(side)
+                nc.scalar.activation(out=side[:], in_=gp[:], func=AF.Relu)
+            elif u == NU - 1 and s2_count[u] % 2 == 1:
+                nc.vector.scalar_tensor_tensor(out=sides[0][:], in0=gp[:], scalar=0.0, in1=sides[0][:],
+                                               op0=ALU.max, op1=ALU.add)
+            elif s2_count[u] == 0:
                 acc_tiles[u] = acc_pool.tile([P, H], F32, name="acc", tag="acc")
                 nc.scalar.activation(out=acc_tiles[u][:], in_=gp[:], func=AF.Relu)
             else:
@@ -332,6 +340,8 @@ def tile_rgat_pa_kernel(tc, adj, x, dmask, W, out):
                                                op0=ALU.max, op1=ALU.add)
             s2_count[u] += 1
             if s2_count[u] == R:
+                if u == NU - 1:
+                    nc.vector.tensor_tensor(out=acc_tiles[u][:], in0=acc_tiles[u][:], in1=sides[0][:], op=ALU.add)
                 nc.sync.dma_start(out=out[b, nt * P:(nt + 1) * P, :], in_=acc_tiles[u][:])
 
         def s2_collect():
@@ -408,12 +418,13 @@ def tile_rgat_pa_kernel(tc, adj, x, dmask, W, out):
             if s2_open:
                 s2_ev()
 
-        make_masks(0)
-        prep_x(0)
+        with tc.manual_schedule(engines={mybir.EngineType.DVE}):
+            h_vector_tick()
+            load_w(1)
+            prep_x(0)
+            h_vector_tick()
+            make_masks(0)
         make_masks(1)
-        h_vector_tick()
-        load_w(1)
-        h_vector_tick()
         prep_x(1)
         h_fill()
         load_adj(1)

@@ -27,7 +27,7 @@ NS_FROM = 10
 S2_PER_STEP = 4
 H_RATE = 3
 HEAD_BANKS = (2, 2, 2, 2, 2, 2, 2, 2, 2, 2, 2, 2)
-FRONT_TICKS = ((1, 0, 1, 0, 0, 0), (0, 1, 0, 0, 0, 0), (0, 0, 1, 0, 0, 0), (1, 0, 0, 1, 0, 0), (1, 0, 1, 0, 1, 1))
+FRONT_TICKS = ((1, 1, 1, 0, 0, 0), (0, 1, 0, 1, 0, 0), (0, 1, 1, 0, 0, 0), (1, 0, 1, 1, 0, 0), (1, 0, 1, 0, 1, 1))
 
 
 def plane_offset(t):
@@ -104,17 +104,11 @@ def tile_rgat_pa_kernel(tc, adj, x, dmask, W, out):
         def make_masks(b):
             mkp = ps_g.tile([P, N], F32, name="mkp", tag="gp")
             nc.tensor.matmul(out=mkp[:], lhsT=ones[:], rhs=zrow[:, b * N:(b + 1) * N], start=True, stop=True)
-            n_e = const.tile([P, 1024], BF16, name="neg_e%d" % b)
-            n_x = const.tile([P, 1024], BF16, name="neg_x%d" % b)
-            n_o = const.tile([P, 1024], BF16, name="neg_o%d" % b)
+            n_x = const.tile([P, 1024], BF16, name="neg%d" % b)
             nc.scalar.activation(out=n_x[:].rearrange("p (m q) -> p m q", q=2),
                                  in_=mkp[:].unsqueeze(2).to_broadcast([P, N, 2]),
                                  func=AF.Copy, scale=-BIG, bias=BIG)
-            both = n_x[:].rearrange("p (mp c q) -> p mp c q", c=2, q=2)
-            for c, dst in ((0, n_e), (1, n_o)):
-                nc.vector.tensor_copy(out=dst[:].rearrange("p (mp d q) -> p mp d q", d=2, q=2),
-                                      in_=both[:, :, c:c + 1, :].to_broadcast([P, 256, 2, 2]))
-            negs.append((n_e, n_x, n_o))
+            negs.append(n_x)
 
         ss = const.tile([P, NU * R], F32, name="ss")
         rs = const.tile([P, NU * R], F32, name="rs")
@@ -203,32 +197,25 @@ def tile_rgat_pa_kernel(tc, adj, x, dmask, W, out):
 
         def front_pieces(u):
             b = u // NT
-            n_e, n_x, n_o = negs[b]
             box = {}
+            neg4 = negs[b][:].rearrange("p (mp q) -> p mp q", q=4)
+            pairs = negs[b][:].rearrange("p (mp c q) -> p mp c q", c=2, q=2)
 
-            def m1():
-                box["av"] = a_tiles[u][:].rearrange("p (mp g) -> p mp g", g=20)
-                lp = l_pool.tile([P, LPW], BF16, name="lp", tag="lp")
-                lp_tiles[u] = lp
-                nc.vector.tensor_tensor(
-                    out=lp[:, 0:2048].rearrange("p (j mp q) -> p j mp q", j=2, q=4),
-                    in0=n_e[:].rearrange("p (mp q) -> p mp q", q=4).unsqueeze(1).to_broadcast([P, 2, 256, 4]),
-                    in1=box["av"][:, :, 0:8].rearrange("p mp (j q) -> p j mp q", j=2),
-                    op=ALU.subtract)
-
-            def m2():
-                nc.vector.tensor_tensor(
-                    out=lp_tiles[u][:, 2048:3072].rearrange("p (mp q) -> p mp q", q=4),
-                    in0=n_x[:].rearrange("p (mp q) -> p mp q", q=4),
-                    in1=box["av"][:, :, 8:12],
-                    op=ALU.subtract)
-
-            def m3():
-                nc.vector.tensor_tensor(
-                    out=lp_tiles[u][:, 3072:5120].rearrange("p (j mp q) -> p j mp q", j=2, q=4),
-                    in0=n_o[:].rearrange("p (mp q) -> p mp q", q=4).unsqueeze(1).to_broadcast([P, 2, 256, 4]),
-                    in1=box["av"][:, :, 12:20].rearrange("p mp (j q) -> p j mp q", j=2),
-                    op=ALU.subtract)
+            def mask(g):
+                def go():
+                    if g == 0:
+                        lp_tiles[u] = l_pool.tile([P, LPW], BF16, name="lp", tag="lp")
+                    av = a_tiles[u][:].rearrange("p (mp g) -> p mp g", g=20)[:, :, 4 * g:4 * g + 4]
+                    dst = lp_tiles[u][:, 1024 * g:1024 * (g + 1)].rearrange("p (mp q) -> p mp q", q=4)
+                    if g == 2:
+                        nc.vector.tensor_tensor(out=dst, in0=neg4, in1=av, op=ALU.subtract)
+                    else:
+                        c = g // 3
+                        nc.vector.tensor_tensor(
+                            out=dst.rearrange("p mp (d q) -> p mp d q", d=2),
+                            in0=pairs[:, :, c:c + 1, :].to_broadcast([P, 256, 2, 2]),
+                            in1=av.rearrange("p mp (d q) -> p mp d q", d=2), op=ALU.subtract)
+                return go
 
             def level(w):
                 def go():
@@ -252,7 +239,7 @@ def tile_rgat_pa_kernel(tc, adj, x, dmask, W, out):
                                         in1=box["tr"][:, 0, 64 + R:64 + 2 * R], op=ALU.min)
                 mn_tiles[u] = mn
 
-            return [m1, m2, m3] + [level(w) for w in (512, 256, 128, 64, 32)] + [tail, fin]
+            return [mask(g) for g in range(5)] + [level(w) for w in (512, 256, 128, 64, 32)] + [tail, fin]
 
         def exp_pair(i):
             u, rp = i // 5, i % 5

@@ -43,10 +43,10 @@ def tile_rgat_pa_kernel(tc, adj, x, dmask, W, out):
         t_pool = ctx.enter_context(tc.tile_pool(name="t_pool", bufs=1))
         st_pool = ctx.enter_context(tc.tile_pool(name="st_pool", bufs=3))
         e_pool = ctx.enter_context(tc.tile_pool(name="e_pool", bufs=E_AHEAD + 1))
-        at_pool = ctx.enter_context(tc.tile_pool(name="at_pool", bufs=3))
+        at_pool = ctx.enter_context(tc.tile_pool(name="at_pool", bufs=5))
         ga_pool = ctx.enter_context(tc.tile_pool(name="ga_pool", bufs=3))
         aq_pool = ctx.enter_context(tc.tile_pool(name="aq_pool", bufs=5))
-        w_pool = ctx.enter_context(tc.tile_pool(name="w_pool", bufs=3))
+        w_pool = ctx.enter_context(tc.tile_pool(name="w_pool", bufs=5))
         gw_pool = ctx.enter_context(tc.tile_pool(name="gw_pool", bufs=2))
         wq_pool = ctx.enter_context(tc.tile_pool(name="wq_pool", bufs=2))
         gh_pool = ctx.enter_context(tc.tile_pool(name="gh_pool", bufs=2))
@@ -279,6 +279,10 @@ def tile_rgat_pa_kernel(tc, adj, x, dmask, W, out):
                 for u in range(2):
                     nc.tensor.transpose(tp[:, rr * 2 + u, :], words[:, u * P:(u + 1) * P], ident32[:])
             tp_tiles[i] = tp
+            if hstate["mm"] == 80:
+                for rr in range(2):
+                    keep = ps_h.tile([P, N], F32, name="keep", tag="hp")
+                    nc.tensor.matmul(out=keep[:], lhsT=ones[:], rhs=at2[:, rr, :], start=True, stop=True)
 
         def att_ev(i):
             ga = ga_pool.tile([P, 1024], BF16, name="ga", tag="ga", align_bytes=64)

@@ -19,7 +19,7 @@ FLOPS = 2 * B * R * N * H * (H + N)
 BIG = 1.0e30
 LPW = 7168
 H_BANKS = 3
-E_AHEAD = 3
+E_AHEAD = 4
 W_AHEAD = 12
 G_BANKS = 3
 W_SCALAR = ()
@@ -265,7 +265,7 @@ def tile_rgat_pa_kernel(tc, adj, x, dmask, W, out):
                 at_tiles[i] = at_pool.tile([P, 2, N], BF16, name="at2", tag="at2")
             at2 = at_tiles[i]
             r = 2 * i + rr
-            if 2 <= i // 5 <= 6 and rr == 1:
+            if 2 <= i // 5 <= 6 and rr == 1 or i // 5 == 4:
                 nc.scalar.activation(out=at2[:, rr, :], in_=e2[:, rr, :], func=AF.Copy, scale=rs[:, r:r + 1])
             else:
                 nc.vector.tensor_scalar(out=at2[:, rr, :], in0=e2[:, rr, :], scalar1=rs[:, r:r + 1],

from contextlib import ExitStack

import concourse.mybir as mybir
from concourse.masks import make_identity

F32 = mybir.dt.float32
BF16 = mybir.dt.bfloat16
U32 = mybir.dt.uint32
U8 = mybir.dt.uint8
FP8X4 = mybir.dt.float8_e4m3fn_x4
ALU = mybir.AluOpType
AF = mybir.ActivationFunctionType

P = 128
B, N, H, R = 2, 512, 512, 10
NT = N // P
NU = B * NT
FLOPS = 2 * B * R * N * H * (H + N)
BIG = 1.0e30
LPW = 7168
H_BANKS = 3
E_AHEAD = 4
W_AHEAD = 12
G_BANKS = 3
W_SCALAR = ()
NS_FROM = 10
S2_PER_STEP = 4
H_RATE = 3
HEAD_BANKS = (2, 2, 2, 2, 2, 2, 2, 2, 2, 2, 2, 2)
FRONT_TICKS = ((1, 1, 1, 0, 0, 0), (0, 1, 0, 1, 0, 0), (0, 1, 1, 0, 0, 0), (1, 0, 1, 1, 0, 0), (1, 0, 1, 0, 1, 1))


def plane_offset(t):
    return (t // 4) * 1024 + t % 4


def tile_rgat_pa_kernel(tc, adj, x, dmask, W, out):
    nc = tc.nc
    with ExitStack() as ctx:
        const = ctx.enter_context(tc.tile_pool(name="const", bufs=1))
        a_pool = ctx.enter_context(tc.tile_pool(name="a_pool", bufs=2))
        l_pool = ctx.enter_context(tc.tile_pool(name="l_pool", bufs=2))
        t_pool = ctx.enter_context(tc.tile_pool(name="t_pool", bufs=1))
        st_pool = ctx.enter_context(tc.tile_pool(name="st_pool", bufs=3))
        e_pool = ctx.enter_context(tc.tile_pool(name="e_pool", bufs=E_AHEAD + 1))
        at_pool = ctx.enter_context(tc.tile_pool(name="at_pool", bufs=5))
        ga_pool = ctx.enter_context(tc.tile_pool(name="ga_pool", bufs=3))
        aq_pool = ctx.enter_context(tc.tile_pool(name="aq_pool", bufs=5))
        w_pool = ctx.enter_context(tc.tile_pool(name="w_pool", bufs=5))
        gw_pool = ctx.enter_context(tc.tile_pool(name="gw_pool", bufs=2))
        wq_pool = ctx.enter_context(tc.tile_pool(name="wq_pool", bufs=2))
        gh_pool = ctx.enter_context(tc.tile_pool(name="gh_pool", bufs=2))
        acc_pool = ctx.enter_context(tc.tile_pool(name="acc_pool", bufs=5))
        ps_h = ctx.enter_context(tc.psum_pool(name="ps_h", bufs=H_BANKS))
        ps_g = ctx.enter_context(tc.psum_pool(name="ps_g", bufs=G_BANKS))
        ps_t = ctx.enter_context(tc.psum_pool(name="ps_t", bufs=2))

        warm = const.tile([P, 1], F32, name="warm")
        nc.vector.memset(warm[:], 0.0)
        nc.scalar.activation(out=warm[:], in_=warm[:], func=AF.Exp)
        ident32 = const.tile([P, P], F32, name="ident32")
        make_identity(nc, ident32[:])

        zrow = const.tile([P, B * N], BF16, name="zrow")
        nc.vector.memset(zrow[:], 0.0)
        ones = const.tile([P, P], BF16, name="ones")
        nc.vector.memset(ones[:], 1.0)

        a_tiles = {}

        def load_adj(u):
            b, nt = u // NT, u % NT
            a_t = a_pool.tile([P, N * R], BF16, name="a_t", tag="a_t")
            nc.sync.dma_start(out=a_t[:], in_=adj[b, nt * P:(nt + 1) * P].rearrange("n m r -> n (m r)"))
            a_tiles[u] = a_t

        w_tiles = {}

        def load_w(r):
            wr = w_pool.tile([P, 4, H], BF16, name="wraw", tag="wraw")
            nc.sync.dma_start(
                out=wr[:].rearrange("p (u e) f -> p u (e f)", u=2),
                in_=W[r].rearrange("(u p e) f -> p u (e f)", u=2, e=2),
            )
            w_tiles[r] = wr

        x_tiles = []

        def load_x(b):
            xr = w_pool.tile([P, 4, H], BF16, name="xraw", tag="wraw")
            nc.sync.dma_start(
                out=xr[:].rearrange("p (a c) k -> p a (c k)", a=2),
                in_=x[b].rearrange("(a p c) k -> p a (c k)", a=2, c=2),
            )
            x_tiles.append(xr)

        load_w(0)
        load_x(0)
        nc.sync.dma_start(out=zrow[0:1, :], in_=dmask.rearrange("b o m -> o (b m)"))
        load_adj(0)
        load_x(1)
        negs = []

        def make_masks(b):
            mkp = ps_g.tile([P, N], F32, name="mkp", tag="gp")
            nc.tensor.matmul(out=mkp[:], lhsT=ones[:], rhs=zrow[:, b * N:(b + 1) * N], start=True, stop=True)
            n_x = const.tile([P, 1024], BF16, name="neg%d" % b)
            nc.scalar.activation(out=n_x[:].rearrange("p (m q) -> p m q", q=2),
                                 in_=mkp[:].unsqueeze(2).to_broadcast([P, N, 2]),
                                 func=AF.Copy, scale=-BIG, bias=BIG)
            negs.append(n_x)

        ss = const.tile([P, NU * R], F32, name="ss")
        rs = const.tile([P, NU * R], F32, name="rs")
        xq, xs = [], []

        def prep_x(b):
            xw = x_tiles[b][:].rearrange("p s k -> p (s k)").bitcast(F32)
            gx = gw_pool.tile([P, H, 4], BF16, name="gx", tag="gw", align_bytes=64)
            gxw = gx[:].rearrange("p f t -> p (f t)").bitcast(F32)
            for q in range(2):
                xt = ps_t.tile([P, 4, P], F32, name="xt", tag="tp")
                for tl in range(2):
                    t = 2 * q + tl
                    for u in range(2):
                        c0 = t * 256 + u * P
                        nc.tensor.transpose(xt[:, tl * 2 + u, :], xw[:, c0:c0 + P], ident32[:])
                nc.scalar.copy(
                    out=gxw[:, q * 512:(q + 1) * 512].rearrange("p (t c u) -> p t c u", t=2, u=2),
                    in_=xt[:].rearrange("p (t u) c -> p t c u", t=2))
            xq_b = const.tile([P, N], U32, name="xq%d" % b, align_bytes=64)
            xs_b = const.tile([P, N], U8, name="xs%d" % b, align_bytes=64)
            nc.vector.quantize_mx(out=xq_b[:].bitcast(FP8X4), scales=xs_b[:],
                                  in_=gx[:].rearrange("p f t -> p (f t)"))
            xq.append(xq_b)
            xs.append(xs_b)

        hq, hs = {}, {}
        wq_tiles, gh_tiles, hp_tiles = {}, {}, {}
        lp_tiles, mn_tiles = {}, {}
        e_tiles, at_tiles, tp_tiles, ga_tiles = {}, {}, {}, {}
        aq_tiles, as_tiles, acc_tiles = {}, {}, {}
        att_done = [set() for u in range(NU)]
        h_done = set()
        s2_seen = set()
        s2_ready = []
        sides = []
        s2_open = []
        s2_count = [0 for u in range(NU)]

        def w_regroup(r):
            gw = gw_pool.tile([P, H, 4], BF16, name="gw", tag="gw", align_bytes=64)
            copy = nc.vector.tensor_copy if r not in W_SCALAR else nc.scalar.copy
            copy(
                out=gw[:].rearrange("p (c i) t -> p c t i", i=4),
                in_=w_tiles[r][:].rearrange("p t (c i) -> p c t i", i=4))
            wq_tiles[r] = [gw]

        def w_quant(r):
            gw = wq_tiles[r][0]
            wq = wq_pool.tile([P, H], U32, name="wq", tag="wq", align_bytes=64)
            ws = wq_pool.tile([P, H], U8, name="ws", tag="ws", align_bytes=64)
            nc.vector.quantize_mx(out=wq[:].bitcast(FP8X4), scales=ws[:],
                                  in_=gw[:].rearrange("p f t -> p (f t)"))
            wq_tiles[r] = [wq, ws]

        def h_mm(g):
            r, b, c = g // 8, (g % 8) // 4, g % 4
            wq, ws = wq_tiles[r]
            hp = ps_h.tile([P, 4, P], F32, name="hp", tag="hp")
            for t in range(4):
                nc.tensor.matmul_mx(
                    out=hp[:, t, :],
                    lhsT=xq[b][:, t * P:(t + 1) * P].bitcast(FP8X4),
                    lhsT_scale=xs[b][:, t * P:(t + 1) * P],
                    rhs=wq[:, c * P:(c + 1) * P].bitcast(FP8X4),
                    rhs_scale=ws[:, c * P:(c + 1) * P],
                    start=True, stop=True)
            hp_tiles[g] = hp

        def h_ev(g):
            r, b, c = g // 8, (g % 8) // 4, g % 4
            if c == 0:
                gh_tiles[(b, r)] = gh_pool.tile([P, 4 * H], BF16, name="gh", tag="gh", align_bytes=64)
            gh = gh_tiles[(b, r)]
            nc.scalar.copy(
                out=gh[:, c * 512:(c + 1) * 512].rearrange("p (f t) -> p f t", t=4),
                in_=hp_tiles[g][:].rearrange("p t f -> p f t"))

        def h_quant(b, r):
            hq_t = const.tile([P, H], U32, name="hq%d_%d" % (b, r), align_bytes=64)
            hs_t = const.tile([P, H], U8, name="hs%d_%d" % (b, r), align_bytes=64)
            nc.vector.quantize_mx(out=hq_t[:].bitcast(FP8X4), scales=hs_t[:], in_=gh_tiles[(b, r)][:])
            hq[(b, r)] = hq_t
            hs[(b, r)] = hs_t
            h_done.add((b, r))

        def front_pieces(u):
            b = u // NT
            box = {}
            neg4 = negs[b][:].rearrange("p (mp q) -> p mp q", q=4)
            pairs = negs[b][:].rearrange("p (mp c q) -> p mp c q", c=2, q=2)

            def mask(g):
                def go():
                    if g == 0:
                        lp_tiles[u] = l_pool.tile([P, LPW], BF16, name="lp", tag="lp")
                    av = a_tiles[u][:].rearrange("p (mp g) -> p mp g", g=20)[:, :, 4 * g:4 * g + 4]
                    dst = lp_tiles[u][:, 1024 * g:1024 * (g + 1)].rearrange("p (mp q) -> p mp q", q=4)
                    if g == 2:
                        nc.vector.tensor_tensor(out=dst, in0=neg4, in1=av, op=ALU.subtract)
                    else:
                        c = g // 3
                        nc.vector.tensor_tensor(
                            out=dst.rearrange("p mp (d q) -> p mp d q", d=2),
                            in0=pairs[:, :, c:c + 1, :].to_broadcast([P, 256, 2, 2]),
                            in1=av.rearrange("p mp (d q) -> p mp d q", d=2), op=ALU.subtract)
                return go

            def level(w):
                def go():
                    if w == 512:
                        box["tr"] = t_pool.tile([P, 5, 512], BF16, name="tr", tag="tr")
                        src = lp_tiles[u][:, 0:5120].rearrange("p (j x) -> p j x", j=5)
                    else:
                        src = box["tr"]
                    nc.vector.tensor_tensor(out=box["tr"][:, :, 0:w], in0=src[:, :, 0:w], in1=src[:, :, w:2 * w],
                                            op=ALU.min)
                return go

            def tail():
                nc.vector.tensor_reduce(out=box["tr"][:, 0, 64:84].rearrange("p (j q) -> p j q", j=5),
                                        in_=box["tr"][:, :, 0:32].rearrange("p j (mp q) -> p j q mp", q=4),
                                        axis=mybir.AxisListType.X, op=ALU.min)

            def fin():
                mn = st_pool.tile([P, R], F32, name="mn", tag="mn")
                nc.vector.tensor_tensor(out=mn[:], in0=box["tr"][:, 0, 64:64 + R],
                                        in1=box["tr"][:, 0, 64 + R:64 + 2 * R], op=ALU.min)
                mn_tiles[u] = mn

            return [mask(g) for g in range(5)] + [level(w) for w in (512, 256, 128, 64, 32)] + [tail, fin]

        def exp_pair(i):
            u, rp = i // 5, i % 5
            e2 = e_pool.tile([P, 2, N], F32, name="e2", tag="e2")
            lp = lp_tiles[u]
            for rr in range(2):
                r = 2 * rp + rr
                base = plane_offset(r)
                step = plane_offset(r + R) - base
                view = lp[:, base:base + 2 * step].rearrange("p (s x) -> p x s", s=2)[:, 0:1024:4, :]
                nc.scalar.activation(
                    out=e2[:, rr, :].rearrange("p (mp s) -> p mp s", s=2), in_=view, func=AF.Exp,
                    bias=mn_tiles[u][:, r:r + 1], scale=-1.0, accum_out=ss[:, 2 * i + rr:2 * i + rr + 1])
            e_tiles[i] = e2

        def recip(i):
            if i % 2 == 0:
                nc.vector.reciprocal(out=rs[:, 2 * i:2 * i + 4], in_=ss[:, 2 * i:2 * i + 4])

        def norm_one(i, rr):
            e2 = e_tiles[i]
            if rr == 0:
                at_tiles[i] = at_pool.tile([P, 2, N], BF16, name="at2", tag="at2")
            at2 = at_tiles[i]
            r = 2 * i + rr
            if 2 <= i // 5 <= 6 and rr == 1 or i // 5 == 4:
                nc.scalar.activation(out=at2[:, rr, :], in_=e2[:, rr, :], func=AF.Copy, scale=rs[:, r:r + 1])
            else:
                nc.vector.tensor_scalar(out=at2[:, rr, :], in0=e2[:, rr, :], scalar1=rs[:, r:r + 1],
                                        scalar2=None, op0=ALU.mult)

        def transposes(i):
            at2 = at_tiles[i]
            tp = ps_t.tile([P, 4, P], F32, name="tp", tag="tp")
            for rr in range(2):
                words = at2[:, rr, :].bitcast(F32)
                for u in range(2):
                    nc.tensor.transpose(tp[:, rr * 2 + u, :], words[:, u * P:(u + 1) * P], ident32[:])
            tp_tiles[i] = tp
            if hstate["mm"] == 80:
                for rr in range(2):
                    keep = ps_h.tile([P, N], F32, name="keep", tag="hp")
                    nc.tensor.matmul(out=keep[:], lhsT=ones[:], rhs=at2[:, rr, :], start=True, stop=True)

        def att_ev(i):
            ga = ga_pool.tile([P, 1024], BF16, name="ga", tag="ga", align_bytes=64)
            nc.scalar.copy(out=ga[:].bitcast(F32).rearrange("p (r n u) -> p r n u", r=2, u=2),
                     in_=tp_tiles[i][:].rearrange("p (r u) n -> p r n u", r=2))
            ga_tiles[i] = ga

        def att_quant(i):
            u, rp = i // 5, i % 5
            if rp == 0:
                aq_tiles[u] = aq_pool.tile([P, R * P], U32, name="aq", tag="aq", align_bytes=64)
                as_tiles[u] = aq_pool.tile([P, R * P], U8, name="asc", tag="asc", align_bytes=64)
            nc.vector.quantize_mx(out=aq_tiles[u][:, rp * 256:(rp + 1) * 256].bitcast(FP8X4),
                                  scales=as_tiles[u][:, rp * 256:(rp + 1) * 256], in_=ga_tiles[i][:])
            att_done[u].add(2 * rp)
            att_done[u].add(2 * rp + 1)

        def s2_mm(u, r):
            b = u // NT
            gp = ps_g.tile([P, H], F32, name="gp", tag="gp")
            nc.tensor.matmul_mx(
                out=gp[:],
                lhsT=aq_tiles[u][:, r * P:(r + 1) * P].bitcast(FP8X4),
                lhsT_scale=as_tiles[u][:, r * P:(r + 1) * P],
                rhs=hq[(b, r)][:].bitcast(FP8X4),
                rhs_scale=hs[(b, r)][:],
                start=True, stop=True)
            s2_open.append((u, r, gp))

        def s2_ev():
            u, r, gp = s2_open.pop(0)
            b, nt = u // NT, u % NT
            if u == NU - 1 and s2_count[u] == 1:
                side = acc_pool.tile([P, H], F32, name="acc", tag="acc")
                sides.append(side)
                nc.scalar.activation(out=side[:], in_=gp[:], func=AF.Relu)
            elif u == NU - 1 and s2_count[u] % 2 == 1:
                nc.vector.scalar_tensor_tensor(out=sides[0][:], in0=gp[:], scalar=0.0, in1=sides[0][:],
                                               op0=ALU.max, op1=ALU.add)
            elif s2_count[u] == 0:
                acc_tiles[u] = acc_pool.tile([P, H], F32, name="acc", tag="acc")
                nc.scalar.activation(out=acc_tiles[u][:], in_=gp[:], func=AF.Relu)
            else:
                acc = acc_tiles[u]
                nc.vector.scalar_tensor_tensor(out=acc[:], in0=gp[:], scalar=0.0, in1=acc[:],
                                               op0=ALU.max, op1=ALU.add)
            s2_count[u] += 1
            if s2_count[u] == R:
                if u == NU - 1:
                    nc.vector.tensor_tensor(out=acc_tiles[u][:], in0=acc_tiles[u][:], in1=sides[0][:], op=ALU.add)
                nc.sync.dma_start(out=out[b, nt * P:(nt + 1) * P, :], in_=acc_tiles[u][:])

        def s2_collect():
            for u in range(NU):
                for r in range(R):
                    if (u, r) not in s2_seen and r in att_done[u] and (u // NT, r) in h_done:
                        s2_seen.add((u, r))
                        s2_ready.append((u, r))

        def s2_drain(late):
            keep = []
            fresh = set()
            while s2_open:
                u = s2_open[0][0]
                if not late and u in fresh:
                    keep.append(s2_open.pop(0))
                    continue
                if s2_count[u] == 0:
                    fresh.add(u)
                s2_ev()
            s2_open.extend(keep)

        def s2_issue(limit):
            s2_collect()
            n = 0
            while s2_ready and n < limit:
                if len(s2_open) == G_BANKS:
                    s2_ev()
                u, r = s2_ready.pop(0)
                s2_mm(u, r)
                n += 1

        hstate = {"mm": 0, "ev": 0, "wr": 0, "wq": 0}
        hq_wait = []
        fq = []

        def front_tick(n=1):
            for q in range(n):
                if fq:
                    fq.pop(0)()

        def h_fill():
            while hstate["mm"] < 80 and hstate["mm"] < hstate["ev"] + H_BANKS and hstate["mm"] // 8 < hstate["wq"]:
                h_mm(hstate["mm"])
                hstate["mm"] += 1

        def h_vector_tick():
            if hq_wait and hq_wait[0][2] <= hstate["ev"]:
                b, r, when = hq_wait.pop(0)
                h_quant(b, r)
            elif hstate["wq"] < hstate["wr"]:
                w_quant(hstate["wq"])
                hstate["wq"] += 1
                h_fill()
            elif hstate["wr"] < R and hstate["wr"] * 8 < hstate["ev"] + W_AHEAD:
                r = hstate["wr"]
                w_regroup(r)
                if r + 2 < R:
                    load_w(r + 2)
                hstate["wr"] += 1

        def h_banks(n):
            for q in range(n):
                g = hstate["ev"]
                if g >= 80 or g >= hstate["mm"]:
                    return
                h_ev(g)
                hstate["ev"] += 1
                h_fill()
                if g % 4 == 3:
                    hq_wait.append(((g % 8) // 4, g // 8, min(g + 2, 80)))

        def s2_one():
            if s2_open:
                s2_ev()

        with tc.manual_schedule(engines={mybir.EngineType.DVE}):
            h_vector_tick()
            load_w(1)
            prep_x(0)
            h_vector_tick()
            make_masks(0)
        make_masks(1)
        prep_x(1)
        h_fill()
        load_adj(1)
        fq.extend(front_pieces(0))
        for q in range(len(HEAD_BANKS)):
            h_banks(HEAD_BANKS[q])
            front_tick()
            h_vector_tick()
        NPAIR = 5 * NU
        for j in range(-E_AHEAD, NPAIR + 3):
            un = (j + E_AHEAD) // 5 + 1
            if (j + E_AHEAD) % 5 == 0 and 0 < un < NU:
                fq.extend(front_pieces(un))
                if un + 1 < NU:
                    load_adj(un + 1)
            nf = FRONT_TICKS[(j + E_AHEAD) % 5]
            if 0 <= j + 1 < NPAIR:
                recip(j + 1)
            front_tick(nf[0])
            s2_one()
            if 0 <= j < NPAIR:
                att_ev(j)
            if 0 <= j - 1 < NPAIR:
                att_quant(j - 1)
            front_tick(nf[1])
            if 0 <= j + 1 < NPAIR:
                norm_one(j + 1, 0)
            s2_one()
            front_tick(nf[2])
            if 0 <= j + 1 < NPAIR:
                norm_one(j + 1, 1)
                transposes(j + 1)
            s2_one()
            s2_issue(S2_PER_STEP)
            if 0 <= j + E_AHEAD < NPAIR:
                exp_pair(j + E_AHEAD)
            front_tick(nf[3])
            h_vector_tick()
            h_banks(H_RATE)
            front_tick(nf[4])
            h_vector_tick()
            front_tick(nf[5])
        while hq_wait:
            h_vector_tick()
        s2_issue(100)
        while s2_open:
            s2_ev()
